import numpy as np
import ml_dtypes


def mxq(x, axis, fmt="e4m3"):
    dtype, down = {"e4m3": (ml_dtypes.float8_e4m3fn, 7), "e5m2": (ml_dtypes.float8_e5m2, 14)}[fmt]
    v = np.moveaxis(np.asarray(x, np.float32).astype(ml_dtypes.bfloat16).astype(np.float64), axis, -1)
    blocks = v.reshape(v.shape[:-1] + (-1, 32))
    amax = np.abs(blocks).max(-1, keepdims=True)
    byte = np.maximum(np.where(amax > 0, np.frexp(amax)[1] - 1 + 127, 0) - down, 1)
    scale = np.exp2(byte - 127.0)
    codes = (blocks / scale).astype(np.float32).astype(dtype).astype(np.float64)
    return np.moveaxis((codes * scale).reshape(v.shape), -1, axis)


WIDE = False


def mx_kscale(k):
    if not WIDE:
        return np.ones(k)
    levels = np.array([10, -10, 5, -5, 0])
    if k % 512:
        return np.exp2(np.random.permutation(np.resize(levels, k // 32))).repeat(32)
    a = np.empty((k // 512, 16))
    for p in range(k // 512):
        a[p, :8] = np.random.permutation(np.resize(levels, 8))
        for g in range(8):
            far = levels[np.abs(levels - a[p, g]) >= 10]
            a[p, g + 8] = far[np.random.randint(len(far))]
    return np.exp2(a.ravel()).repeat(32)


BF16 = ml_dtypes.bfloat16


def bf(x):
    return np.asarray(x, np.float32).astype(BF16)


def f64(x):
    return np.asarray(x).astype(np.float64)


B, S, D, H, DH = 4, 2048, 512, 2, 64
ROPE_BASE = 10000.0


def rope_tables():
    inv_freq = 1.0 / ROPE_BASE ** (np.arange(0, DH, 2) / DH)
    freqs = np.arange(S)[:, None] * inv_freq[None, :]
    emb = np.concatenate([freqs, freqs], axis=-1)
    return np.cos(emb), np.sin(emb)


def rotate_half(t):
    t1, t2 = t[..., : DH // 2], t[..., DH // 2 :]
    return np.concatenate([-t2, t1], axis=-1)


def setup_inputs():
    s = mx_kscale(D)
    c, sn = rope_tables()
    return {"x": bf(np.random.standard_normal((B, S, D)) * s),
            "Wq": bf(np.random.standard_normal((H * DH, D)) / np.sqrt(D) / s[None, :]),
            "Wk": bf(np.random.standard_normal((H * DH, D)) / np.sqrt(D) / s[None, :]),
            "rope_cos": bf(c), "rope_sin": bf(sn)}


def reference(x, Wq, Wk, rope_cos, rope_sin):
    xq = mxq(f64(x), 2, "e4m3")
    cos = f64(rope_cos)[None, None]
    sin = f64(rope_sin)[None, None]

    def proj(W):
        y = xq @ mxq(f64(W), 1, "e4m3").T
        return y.reshape(B, S, H, DH).transpose(0, 2, 1, 3)

    q, k = proj(Wq), proj(Wk)
    q_rot = q * cos + rotate_half(q) * sin
    k_rot = k * cos + rotate_half(k) * sin
    return q_rot, k_rot

@@ -1,0 +1,165 @@
+from contextlib import ExitStack
+
+import concourse.mybir as mybir
+from concourse.masks import make_identity
+
+F32 = mybir.dt.float32
+BF16 = mybir.dt.bfloat16
+U32 = mybir.dt.uint32
+U8 = mybir.dt.uint8
+FP8X4 = mybir.dt.float8_e4m3fn_x4
+MULT = mybir.AluOpType.mult
+ADD = mybir.AluOpType.add
+
+P = 128
+PACK = 4
+B, S, D = 4, 2048, 512
+HEADS, DH = 2, 64
+HALF = DH // 2
+GROUPS = 2 * HEADS
+FEATURES = GROUPS * DH
+SLOTS = S // P
+WORDS = D // 2
+CHUNK = 4
+CHUNKS_PER_BATCH = SLOTS // CHUNK
+N_CHUNKS = B * CHUNKS_PER_BATCH
+
+FLOPS = 2 * B * S * D * FEATURES
+
+
+def tile_attention_pa_t_kernel(tc, x, Wq, Wk, rope_cos, rope_sin, out_0, out_1):
+    nc = tc.nc
+    with ExitStack() as stack:
+        const = stack.enter_context(tc.tile_pool(name="const", bufs=1))
+        x_pool = stack.enter_context(tc.tile_pool(name="x", bufs=N_CHUNKS))
+        res_pool = stack.enter_context(tc.tile_pool(name="res", bufs=N_CHUNKS))
+        grouped_pool = stack.enter_context(tc.tile_pool(name="grouped", bufs=3))
+        codes_pool = stack.enter_context(tc.tile_pool(name="codes", bufs=2))
+        prod_pool = stack.enter_context(tc.tile_pool(name="prod", bufs=3))
+        xt_psum = stack.enter_context(tc.psum_pool(name="xt_psum", bufs=4))
+        y_psum = stack.enter_context(tc.psum_pool(name="y_psum", bufs=4))
+        stack.enter_context(tc.manual_schedule())
+
+        def chunk_place(c):
+            return c // CHUNKS_PER_BATCH, (c % CHUNKS_PER_BATCH) * CHUNK
+
+        def load_chunk(c):
+            b, t0 = chunk_place(c)
+            x_sb = x_pool.tile([P, CHUNK * D], BF16)
+            rows = x[b].rearrange("(p t) d -> p (t d)", t=SLOTS)
+            nc.sync.dma_start(out=x_sb[:], in_=rows[:, t0 * D : (t0 + CHUNK) * D])
+            return x_sb
+
+        def transpose_words(bank, rows_sb, first_word, column):
+            words = rows_sb[:].bitcast(F32)
+            for u in range(2):
+                nc.tensor.transpose(
+                    bank[:, u, column : column + P],
+                    words[:, first_word + u : first_word + WORDS : 2],
+                    ident[:],
+                )
+
+        def transpose_chunk(x_sb):
+            grouped = grouped_pool.tile([P, CHUNK * P * PACK], BF16, align_bytes=64)
+            grouped_words = grouped[:].bitcast(F32).rearrange("p (n u) -> p n u", u=2)
+            for pair in range(CHUNK // 2):
+                bank = xt_psum.tile([P, 2, 2 * P], F32, tag="xt")
+                for i in range(2):
+                    transpose_words(bank, x_sb, (2 * pair + i) * WORDS, i * P)
+                nc.scalar.copy(
+                    out=grouped_words[:, pair * 2 * P : (pair + 1) * 2 * P, :],
+                    in_=bank[:].rearrange("p u n -> p n u"),
+                )
+            return grouped
+
+        def quantise_chunk(grouped):
+            x_codes = codes_pool.tile([P, CHUNK * P], U32, align_bytes=64)
+            x_scales = codes_pool.tile([P, CHUNK * P], U8, align_bytes=64)
+            nc.vector.quantize_mx(
+                out=x_codes[:].bitcast(FP8X4), scales=x_scales[:], in_=grouped[:]
+            )
+            return x_codes, x_scales
+
+        def project_tile(x_mx, i):
+            x_codes, x_scales = x_mx
+            tokens = slice(i * P, (i + 1) * P)
+            y = y_psum.tile([P, 2 * FEATURES], F32)
+            nc.tensor.matmul_mx(
+                out=y[:],
+                lhsT=x_codes[:, tokens].bitcast(FP8X4),
+                lhsT_scale=x_scales[:, tokens],
+                rhs=w_codes[:].bitcast(FP8X4),
+                rhs_scale=w_scales[:],
+                start=True,
+                stop=True,
+            )
+            return y
+
+        def multiply_tile(y, t, products, i):
+            nc.vector.tensor_tensor(
+                out=products[:, :, :, i, :],
+                in0=y[:].rearrange("p (c g j) -> p c g j", c=2, g=GROUPS),
+                in1=tables[:, :, t, :].unsqueeze(2).to_broadcast([P, 2, GROUPS, DH]),
+                op=MULT,
+            )
+
+        def store_chunk(c, res):
+            b, t0 = chunk_place(c)
+            for o, out in enumerate((out_0, out_1)):
+                rows = out[b].rearrange("h (p t) j -> p h t j", t=SLOTS)
+                nc.sync.dma_start(
+                    out=rows[:, :, t0 : t0 + CHUNK, :], in_=res[:, o * HEADS : (o + 1) * HEADS, :, :]
+                )
+
+        ident = const.tile([P, P], F32)
+        make_identity(nc, ident[:])
+        wq_sb = const.tile([P, D], BF16)
+        nc.sync.dma_start(out=wq_sb[:], in_=Wq)
+        wk_sb = const.tile([P, D], BF16)
+        nc.sync.dma_start(out=wk_sb[:], in_=Wk)
+        x_tiles = [load_chunk(0), load_chunk(1)]
+        tables = const.tile([P, 2, SLOTS, DH], BF16)
+        nc.sync.dma_start(out=tables[:, 0, :, :], in_=rope_cos.rearrange("(p t) j -> p t j", t=SLOTS))
+        nc.sync.dma_start(out=tables[:, 1, :, :], in_=rope_sin.rearrange("(p t) j -> p t j", t=SLOTS))
+        for c in range(2, N_CHUNKS):
+            x_tiles.append(load_chunk(c))
+
+        w_bank = xt_psum.tile([P, 2, 2 * P], F32, tag="xt")
+        transpose_words(w_bank, wq_sb, 0, 0)
+        transpose_words(w_bank, wk_sb, 0, P)
+        w_grouped = const.tile([P, 2 * FEATURES * PACK], BF16, align_bytes=64)
+        w_words = w_grouped[:].bitcast(F32).rearrange("p (n u) -> p n u", u=2)
+        nc.vector.tensor_copy(out=w_words[:, 0:FEATURES, :], in_=w_bank[:].rearrange("p u n -> p n u"))
+        swapped = w_words[:, FEATURES : 2 * FEATURES, :].rearrange(
+            "p (g a j) u -> p g a j u", g=GROUPS, a=2
+        )
+        straight = w_bank[:].rearrange("p u (g a j) -> p g a j u", g=GROUPS, a=2)
+        for a in range(2):
+            nc.vector.tensor_copy(out=swapped[:, :, a, :, :], in_=straight[:, :, 1 - a, :, :])
+        w_codes = const.tile([P, 2 * FEATURES], U32, align_bytes=64)
+        w_scales = const.tile([P, 2 * FEATURES], U8, align_bytes=64)
+        nc.vector.quantize_mx(out=w_codes[:].bitcast(FP8X4), scales=w_scales[:], in_=w_grouped[:])
+
+        x_mx = quantise_chunk(transpose_chunk(x_tiles[0]))
+        nc.vector.tensor_scalar_mul(
+            out=tables[:, 1, :, 0:HALF], in0=tables[:, 1, :, 0:HALF], scalar1=-1.0
+        )
+        grouped_next = transpose_chunk(x_tiles[1])
+        y_tiles = [project_tile(x_mx, i) for i in range(CHUNK)]
+        for c in range(N_CHUNKS):
+            if c + 1 < N_CHUNKS:
+                x_mx = quantise_chunk(grouped_next)
+            if c + 2 < N_CHUNKS:
+                grouped_next = transpose_chunk(x_tiles[c + 2])
+            products = prod_pool.tile([P, 2, GROUPS, CHUNK, DH], F32)
+            first_slot = chunk_place(c)[1]
+            for i in range(CHUNK):
+                multiply_tile(y_tiles[i], first_slot + i, products, i)
+                if c + 1 < N_CHUNKS:
+                    y_tiles[i] = project_tile(x_mx, i)
+            adder = nc.vector if c == N_CHUNKS - 1 else nc.gpsimd
+            res = res_pool.tile([P, GROUPS, CHUNK, DH], F32)
+            adder.tensor_tensor(
+                out=res[:], in0=products[:, 0, :, :, :], in1=products[:, 1, :, :, :], op=ADD
+            )
+            store_chunk(c, res)

@@ -80,28 +80,38 @@ def tile_attention_pa_t_kernel(tc, x, Wq, Wk, rope_cos, rope_sin, out_0, out_1):
             )
             return x_codes, x_scales
 
-        def project_tile(x_mx, i):
+        def project_pair(x_mx, pair):
             x_codes, x_scales = x_mx
-            tokens = slice(i * P, (i + 1) * P)
             y = y_psum.tile([P, 2 * FEATURES], F32)
-            nc.tensor.matmul_mx(
-                out=y[:],
-                lhsT=x_codes[:, tokens].bitcast(FP8X4),
-                lhsT_scale=x_scales[:, tokens],
-                rhs=w_codes[:].bitcast(FP8X4),
-                rhs_scale=w_scales[:],
-                start=True,
-                stop=True,
-            )
+            for i in range(2):
+                tokens = slice((2 * pair + i) * P, (2 * pair + i + 1) * P)
+                nc.tensor.matmul_mx(
+                    out=y[:, i * FEATURES : (i + 1) * FEATURES],
+                    lhsT=x_codes[:, tokens].bitcast(FP8X4),
+                    lhsT_scale=x_scales[:, tokens],
+                    rhs=w_codes[:].bitcast(FP8X4),
+                    rhs_scale=w_scales[:],
+                    start=True,
+                    stop=True,
+                )
             return y
 
-        def multiply_tile(y, t, products, i):
+        def multiply_pair(y, t, products, i):
+            tiles = slice(i, i + 2)
             nc.vector.tensor_tensor(
-                out=products[:, :, :, i, :],
-                in0=y[:].rearrange("p (c g j) -> p c g j", c=2, g=GROUPS),
-                in1=tables[:, :, t, :].unsqueeze(2).to_broadcast([P, 2, GROUPS, DH]),
+                out=products[:, 0, :, tiles, :].rearrange("p g i j -> p i g j"),
+                in0=y[:].rearrange("p (i g j) -> p i g j", i=2, g=GROUPS),
+                in1=tables[:, 0, t : t + 2, :].unsqueeze(2).to_broadcast([P, 2, GROUPS, DH]),
                 op=MULT,
             )
+            for a in range(2):
+                half = slice(a * HALF, (a + 1) * HALF)
+                nc.vector.tensor_tensor(
+                    out=products[:, 1, :, tiles, half].rearrange("p g i j -> p i g j"),
+                    in0=y[:].rearrange("p (i g a j) -> p i g a j", i=2, g=GROUPS, a=2)[:, :, :, 1 - a, :],
+                    in1=tables[:, 1, t : t + 2, half].unsqueeze(2).to_broadcast([P, 2, GROUPS, HALF]),
+                    op=MULT,
+                )
 
         def store_chunk(c, res):
             b, t0 = chunk_place(c)
@@ -127,17 +137,11 @@ def tile_attention_pa_t_kernel(tc, x, Wq, Wk, rope_cos, rope_sin, out_0, out_1):
         w_bank = xt_psum.tile([P, 2, 2 * P], F32, tag="xt")
         transpose_words(w_bank, wq_sb, 0, 0)
         transpose_words(w_bank, wk_sb, 0, P)
-        w_grouped = const.tile([P, 2 * FEATURES * PACK], BF16, align_bytes=64)
+        w_grouped = const.tile([P, FEATURES * PACK], BF16, align_bytes=64)
         w_words = w_grouped[:].bitcast(F32).rearrange("p (n u) -> p n u", u=2)
-        nc.vector.tensor_copy(out=w_words[:, 0:FEATURES, :], in_=w_bank[:].rearrange("p u n -> p n u"))
-        swapped = w_words[:, FEATURES : 2 * FEATURES, :].rearrange(
-            "p (g a j) u -> p g a j u", g=GROUPS, a=2
-        )
-        straight = w_bank[:].rearrange("p u (g a j) -> p g a j u", g=GROUPS, a=2)
-        for a in range(2):
-            nc.vector.tensor_copy(out=swapped[:, :, a, :, :], in_=straight[:, :, 1 - a, :, :])
-        w_codes = const.tile([P, 2 * FEATURES], U32, align_bytes=64)
-        w_scales = const.tile([P, 2 * FEATURES], U8, align_bytes=64)
+        nc.vector.tensor_copy(out=w_words, in_=w_bank[:].rearrange("p u n -> p n u"))
+        w_codes = const.tile([P, FEATURES], U32, align_bytes=64)
+        w_scales = const.tile([P, FEATURES], U8, align_bytes=64)
         nc.vector.quantize_mx(out=w_codes[:].bitcast(FP8X4), scales=w_scales[:], in_=w_grouped[:])
 
         x_mx = quantise_chunk(transpose_chunk(x_tiles[0]))
@@ -145,7 +149,7 @@ def tile_attention_pa_t_kernel(tc, x, Wq, Wk, rope_cos, rope_sin, out_0, out_1):
             out=tables[:, 1, :, 0:HALF], in0=tables[:, 1, :, 0:HALF], scalar1=-1.0
         )
         grouped_next = transpose_chunk(x_tiles[1])
-        y_tiles = [project_tile(x_mx, i) for i in range(CHUNK)]
+        y_next = [project_pair(x_mx, pair) for pair in range(CHUNK // 2)]
         for c in range(N_CHUNKS):
             if c + 1 < N_CHUNKS:
                 x_mx = quantise_chunk(grouped_next)
@@ -153,10 +157,11 @@ def tile_attention_pa_t_kernel(tc, x, Wq, Wk, rope_cos, rope_sin, out_0, out_1):
                 grouped_next = transpose_chunk(x_tiles[c + 2])
             products = prod_pool.tile([P, 2, GROUPS, CHUNK, DH], F32)
             first_slot = chunk_place(c)[1]
-            for i in range(CHUNK):
-                multiply_tile(y_tiles[i], first_slot + i, products, i)
-                if c + 1 < N_CHUNKS:
-                    y_tiles[i] = project_tile(x_mx, i)
+            y_pairs = y_next
+            if c + 1 < N_CHUNKS:
+                y_next = [project_pair(x_mx, pair) for pair in range(CHUNK // 2)]
+            for pair in range(CHUNK // 2):
+                multiply_pair(y_pairs[pair], first_slot + 2 * pair, products, 2 * pair)
             adder = nc.vector if c == N_CHUNKS - 1 else nc.gpsimd
             res = res_pool.tile([P, GROUPS, CHUNK, DH], F32)
             adder.tensor_tensor(

@@ -23,6 +23,7 @@ WORDS = D // 2
 CHUNK = 4
 CHUNKS_PER_BATCH = SLOTS // CHUNK
 N_CHUNKS = B * CHUNKS_PER_BATCH
+LAST = CHUNK - 1
 
 FLOPS = 2 * B * S * D * FEATURES
 
@@ -36,12 +37,17 @@ def tile_attention_pa_t_kernel(tc, x, Wq, Wk, rope_cos, rope_sin, out_0, out_1):
         grouped_pool = stack.enter_context(tc.tile_pool(name="grouped", bufs=3))
         codes_pool = stack.enter_context(tc.tile_pool(name="codes", bufs=2))
         prod_pool = stack.enter_context(tc.tile_pool(name="prod", bufs=3))
-        xt_psum = stack.enter_context(tc.psum_pool(name="xt_psum", bufs=4))
-        y_psum = stack.enter_context(tc.psum_pool(name="y_psum", bufs=4))
+        prod_t_pool = stack.enter_context(tc.tile_pool(name="prod_t", bufs=2))
+        xt_psum = stack.enter_context(tc.psum_pool(name="xt_psum", bufs=3))
+        y_psum = stack.enter_context(tc.psum_pool(name="y_psum", bufs=CHUNK))
+        sum_psum = stack.enter_context(tc.psum_pool(name="sum_psum", bufs=1))
         stack.enter_context(tc.manual_schedule())
 
         def chunk_place(c):
             return c // CHUNKS_PER_BATCH, (c % CHUNKS_PER_BATCH) * CHUNK
+
+        def has_turned(c):
+            return c > 0
 
         def load_chunk(c):
             b, t0 = chunk_place(c)
@@ -80,37 +86,99 @@ def tile_attention_pa_t_kernel(tc, x, Wq, Wk, rope_cos, rope_sin, out_0, out_1):
             )
             return x_codes, x_scales
 
-        def project_pair(x_mx, pair):
+        def project_straight(x_mx, y_cols, i):
             x_codes, x_scales = x_mx
-            y = y_psum.tile([P, 2 * FEATURES], F32)
-            for i in range(2):
-                tokens = slice((2 * pair + i) * P, (2 * pair + i + 1) * P)
+            tokens = slice(i * P, (i + 1) * P)
+            nc.tensor.matmul_mx(
+                out=y_cols,
+                lhsT=x_codes[:, tokens].bitcast(FP8X4),
+                lhsT_scale=x_scales[:, tokens],
+                rhs=w_codes[:].bitcast(FP8X4),
+                rhs_scale=w_scales[:],
+                start=True,
+                stop=True,
+            )
+
+        def project_turned(x_mx, y_cols, i):
+            x_codes, x_scales = x_mx
+            tokens = slice(i * P, (i + 1) * P)
+            for o in range(2):
+                rows = slice(o * P, (o + 1) * P)
                 nc.tensor.matmul_mx(
-                    out=y[:, i * FEATURES : (i + 1) * FEATURES],
-                    lhsT=x_codes[:, tokens].bitcast(FP8X4),
-                    lhsT_scale=x_scales[:, tokens],
-                    rhs=w_codes[:].bitcast(FP8X4),
-                    rhs_scale=w_scales[:],
+                    out=y_cols[:, rows],
+                    lhsT=w_codes[:, rows].bitcast(FP8X4),
+                    lhsT_scale=w_scales[:, rows],
+                    rhs=x_codes[:, tokens].bitcast(FP8X4),
+                    rhs_scale=x_scales[:, tokens],
                     start=True,
                     stop=True,
                 )
-            return y
 
-        def multiply_pair(y, t, products, i):
-            tiles = slice(i, i + 2)
+        def project_chunk(c, x_mx):
+            back = y_psum.tile([P, 2 * FEATURES], F32, name="y")
+            if has_turned(c):
+                project_turned(x_mx, back[:, FEATURES : 2 * FEATURES], LAST)
+            else:
+                project_straight(x_mx, back[:, FEATURES : 2 * FEATURES], LAST)
+            project_straight(x_mx, back[:, 0:FEATURES], LAST - 1)
+            front = y_psum.tile([P, 2 * FEATURES], F32, name="y")
+            for i in range(2):
+                project_straight(x_mx, front[:, i * FEATURES : (i + 1) * FEATURES], i)
+            return front, back
+
+        def multiply_straight(y_cols, n, t, products, i):
             nc.vector.tensor_tensor(
-                out=products[:, 0, :, tiles, :].rearrange("p g i j -> p i g j"),
-                in0=y[:].rearrange("p (i g j) -> p i g j", i=2, g=GROUPS),
-                in1=tables[:, 0, t : t + 2, :].unsqueeze(2).to_broadcast([P, 2, GROUPS, DH]),
+                out=products[:, 0, :, i : i + n, :].rearrange("p g i j -> p i g j"),
+                in0=y_cols.rearrange("p (i g j) -> p i g j", i=n, g=GROUPS),
+                in1=tables[:, 0, t : t + n, :].unsqueeze(2).to_broadcast([P, n, GROUPS, DH]),
                 op=MULT,
             )
-            for a in range(2):
-                half = slice(a * HALF, (a + 1) * HALF)
-                nc.vector.tensor_tensor(
-                    out=products[:, 1, :, tiles, half].rearrange("p g i j -> p i g j"),
-                    in0=y[:].rearrange("p (i g a j) -> p i g a j", i=2, g=GROUPS, a=2)[:, :, :, 1 - a, :],
-                    in1=tables[:, 1, t : t + 2, half].unsqueeze(2).to_broadcast([P, 2, GROUPS, HALF]),
-                    op=MULT,
+            nc.vector.tensor_tensor(
+                out=products[:, 1, :, i : i + n, :].rearrange("p g i (a j) -> p i g a j", a=2),
+                in0=y_cols.rearrange("p (i g a j) -> p i g a j", i=n, g=GROUPS, a=2)[:, :, :, ::-1, :],
+                in1=tables[:, 1, t : t + n, :]
+                .rearrange("p i (a j) -> p i a j", a=2)
+                .unsqueeze(2)
+                .to_broadcast([P, n, GROUPS, 2, HALF]),
+                op=MULT,
+            )
+
+        def multiply_turned(y_cols, chunk_in_batch):
+            prod_t = prod_t_pool.tile([P, 2, 2, P], F32)
+            nc.vector.tensor_tensor(
+                out=prod_t[:],
+                in0=y_cols.rearrange("p (o n) -> p o n", o=2).unsqueeze(1).to_broadcast([P, 2, 2, P]),
+                in1=tables_t[:, chunk_in_batch, :, :].unsqueeze(2).to_broadcast([P, 2, 2, P]),
+                op=MULT,
+            )
+            return prod_t
+
+        def add_turned(prod_t, res):
+            total = sum_psum.tile([P, FEATURES], F32)
+            for o in range(2):
+                for c, moving in enumerate((ident, swap)):
+                    nc.tensor.matmul(
+                        out=total[:, o * P : (o + 1) * P],
+                        lhsT=prod_t[:, c, o, :],
+                        rhs=moving[:],
+                        start=c == 0,
+                        stop=c == 1,
+                        is_transpose=True,
+                    )
+            nc.scalar.copy(out=res[:, :, LAST, :], in_=total[:].rearrange("p (g j) -> p g j", g=GROUPS))
+
+        def transpose_tables():
+            for n2 in range(CHUNKS_PER_BATCH // 2):
+                bank = xt_psum.tile([P, 2, 2 * P], F32, tag="xt")
+                for i in range(2):
+                    for plane in range(2):
+                        nc.tensor.transpose(
+                            bank[:, i, plane * P : (plane + 1) * P],
+                            spread[:, 2 * n2 + i, plane, :, :].rearrange("p h j -> p (h j)"),
+                            ident[:],
+                        )
+                nc.scalar.copy(
+                    out=tables_t[:, 2 * n2 : 2 * n2 + 2, :, :].rearrange("p n c r -> p n (c r)"), in_=bank[:]
                 )
 
         def store_chunk(c, res):
@@ -123,6 +191,12 @@ def tile_attention_pa_t_kernel(tc, x, Wq, Wk, rope_cos, rope_sin, out_0, out_1):
 
         ident = const.tile([P, P], F32)
         make_identity(nc, ident[:])
+        swap = const.tile([P, P], F32)
+        for a in range(2):
+            nc.gpsimd.tensor_copy(
+                out=swap[:].rearrange("p (h a j) -> p h a j", h=HEADS, a=2)[:, :, a, :],
+                in_=ident[:].rearrange("p (h a j) -> p h a j", h=HEADS, a=2)[:, :, 1 - a, :],
+            )
         wq_sb = const.tile([P, D], BF16)
         nc.sync.dma_start(out=wq_sb[:], in_=Wq)
         wk_sb = const.tile([P, D], BF16)
@@ -145,26 +219,51 @@ def tile_attention_pa_t_kernel(tc, x, Wq, Wk, rope_cos, rope_sin, out_0, out_1):
         nc.vector.quantize_mx(out=w_codes[:].bitcast(FP8X4), scales=w_scales[:], in_=w_grouped[:])
 
         x_mx = quantise_chunk(transpose_chunk(x_tiles[0]))
-        nc.vector.tensor_scalar_mul(
-            out=tables[:, 1, :, 0:HALF], in0=tables[:, 1, :, 0:HALF], scalar1=-1.0
+        nc.gpsimd.tensor_scalar(
+            out=tables[:, 1, :, 0:HALF], in0=tables[:, 1, :, 0:HALF], scalar1=-1.0, scalar2=0.0, op0=MULT, op1=ADD
         )
+        spread = const.tile([P, CHUNKS_PER_BATCH, 2, HEADS, DH], F32)
+        last_slots = tables[:].rearrange("p c (n i) j -> p c n i j", i=CHUNK)[:, :, :, LAST, :]
+        for plane, source, target in ((0, 0, 0), (1, 0, HALF), (1, HALF, 0)):
+            width = DH if plane == 0 else HALF
+            nc.gpsimd.tensor_scalar(
+                out=spread[:, :, plane, :, target : target + width],
+                in0=last_slots[:, plane, :, source : source + width]
+                .unsqueeze(2)
+                .to_broadcast([P, CHUNKS_PER_BATCH, HEADS, width]),
+                scalar1=1.0,
+                scalar2=0.0,
+                op0=MULT,
+                op1=ADD,
+            )
+        tables_t = const.tile([P, CHUNKS_PER_BATCH, 2, P], F32)
         grouped_next = transpose_chunk(x_tiles[1])
-        y_next = [project_pair(x_mx, pair) for pair in range(CHUNK // 2)]
+        y_next = project_chunk(0, x_mx)
         for c in range(N_CHUNKS):
             if c + 1 < N_CHUNKS:
                 x_mx = quantise_chunk(grouped_next)
             if c + 2 < N_CHUNKS:
                 grouped_next = transpose_chunk(x_tiles[c + 2])
-            products = prod_pool.tile([P, 2, GROUPS, CHUNK, DH], F32)
-            first_slot = chunk_place(c)[1]
-            y_pairs = y_next
+            if c == 0:
+                transpose_tables()
+            front, back = y_next
             if c + 1 < N_CHUNKS:
-                y_next = [project_pair(x_mx, pair) for pair in range(CHUNK // 2)]
-            for pair in range(CHUNK // 2):
-                multiply_pair(y_pairs[pair], first_slot + 2 * pair, products, 2 * pair)
-            adder = nc.vector if c == N_CHUNKS - 1 else nc.gpsimd
+                y_next = project_chunk(c + 1, x_mx)
+            products = prod_pool.tile([P, 2, GROUPS, CHUNK, DH], F32)
             res = res_pool.tile([P, GROUPS, CHUNK, DH], F32)
+            first_slot = chunk_place(c)[1]
+            straight = LAST if has_turned(c) else CHUNK
+            if has_turned(c):
+                prod_t = multiply_turned(back[:, FEATURES : 2 * FEATURES], c % CHUNKS_PER_BATCH)
+                add_turned(prod_t, res)
+            n_back = straight - 2
+            multiply_straight(back[:, 0 : n_back * FEATURES], n_back, first_slot + 2, products, 2)
+            multiply_straight(front[:], 2, first_slot, products, 0)
+            adder = nc.vector if c == N_CHUNKS - 1 else nc.gpsimd
             adder.tensor_tensor(
-                out=res[:], in0=products[:, 0, :, :, :], in1=products[:, 1, :, :, :], op=ADD
+                out=res[:, :, 0:straight, :],
+                in0=products[:, 0, :, 0:straight, :],
+                in1=products[:, 1, :, 0:straight, :],
+                op=ADD,
             )
             store_chunk(c, res)

@@ -21,9 +21,15 @@ FEATURES = GROUPS * DH
 SLOTS = S // P
 WORDS = D // 2
 CHUNK = 4
-CHUNKS_PER_BATCH = SLOTS // CHUNK
-N_CHUNKS = B * CHUNKS_PER_BATCH
-LAST = CHUNK - 1
+CHUNKS = (
+    [(0, t, 2) for t in range(0, 8, 2)]
+    + [(b, t, CHUNK) for b in range(B) for t in range(0, SLOTS, CHUNK)][2:-1]
+    + [(B - 1, t, 2) for t in (SLOTS - 2, SLOTS - 4)]
+)
+N_CHUNKS = len(CHUNKS)
+TURNED = SLOTS // CHUNK
+AHEAD = 3
+FIRST_TURNED = 4
 
 FLOPS = 2 * B * S * D * FEATURES
 
@@ -34,7 +40,7 @@ def tile_attention_pa_t_kernel(tc, x, Wq, Wk, rope_cos, rope_sin, out_0, out_1):
         const = stack.enter_context(tc.tile_pool(name="const", bufs=1))
         x_pool = stack.enter_context(tc.tile_pool(name="x", bufs=N_CHUNKS))
         res_pool = stack.enter_context(tc.tile_pool(name="res", bufs=N_CHUNKS))
-        grouped_pool = stack.enter_context(tc.tile_pool(name="grouped", bufs=3))
+        grouped_pool = stack.enter_context(tc.tile_pool(name="grouped", bufs=AHEAD + 1))
         codes_pool = stack.enter_context(tc.tile_pool(name="codes", bufs=2))
         prod_pool = stack.enter_context(tc.tile_pool(name="prod", bufs=3))
         prod_t_pool = stack.enter_context(tc.tile_pool(name="prod_t", bufs=2))
@@ -43,18 +49,16 @@ def tile_attention_pa_t_kernel(tc, x, Wq, Wk, rope_cos, rope_sin, out_0, out_1):
         sum_psum = stack.enter_context(tc.psum_pool(name="sum_psum", bufs=1))
         stack.enter_context(tc.manual_schedule())
 
-        def chunk_place(c):
-            return c // CHUNKS_PER_BATCH, (c % CHUNKS_PER_BATCH) * CHUNK
-
         def has_turned(c):
-            return c > 0
+            t0, n = CHUNKS[c][1:]
+            return c >= FIRST_TURNED and (t0 + n) % CHUNK == 0
 
         def load_chunk(c):
-            b, t0 = chunk_place(c)
+            b, t0, n = CHUNKS[c]
             x_sb = x_pool.tile([P, CHUNK * D], BF16)
             rows = x[b].rearrange("(p t) d -> p (t d)", t=SLOTS)
-            nc.sync.dma_start(out=x_sb[:], in_=rows[:, t0 * D : (t0 + CHUNK) * D])
-            return x_sb
+            nc.sync.dma_start(out=x_sb[:, 0 : n * D], in_=rows[:, t0 * D : (t0 + n) * D])
+            x_tiles.append(x_sb)
 
         def transpose_words(bank, rows_sb, first_word, column):
             words = rows_sb[:].bitcast(F32)
@@ -65,24 +69,27 @@ def tile_attention_pa_t_kernel(tc, x, Wq, Wk, rope_cos, rope_sin, out_0, out_1):
                     ident[:],
                 )
 
-        def transpose_chunk(x_sb):
+        def transpose_chunk(c):
             grouped = grouped_pool.tile([P, CHUNK * P * PACK], BF16, align_bytes=64)
             grouped_words = grouped[:].bitcast(F32).rearrange("p (n u) -> p n u", u=2)
-            for pair in range(CHUNK // 2):
+            for pair in range(CHUNKS[c][2] // 2):
                 bank = xt_psum.tile([P, 2, 2 * P], F32, tag="xt")
                 for i in range(2):
-                    transpose_words(bank, x_sb, (2 * pair + i) * WORDS, i * P)
+                    transpose_words(bank, x_tiles[c], (2 * pair + i) * WORDS, i * P)
                 nc.scalar.copy(
                     out=grouped_words[:, pair * 2 * P : (pair + 1) * 2 * P, :],
                     in_=bank[:].rearrange("p u n -> p n u"),
                 )
             return grouped
 
-        def quantise_chunk(grouped):
+        def quantise_chunk(c, grouped):
             x_codes = codes_pool.tile([P, CHUNK * P], U32, align_bytes=64)
             x_scales = codes_pool.tile([P, CHUNK * P], U8, align_bytes=64)
+            tokens = CHUNKS[c][2] * P
             nc.vector.quantize_mx(
-                out=x_codes[:].bitcast(FP8X4), scales=x_scales[:], in_=grouped[:]
+                out=x_codes[:, 0:tokens].bitcast(FP8X4),
+                scales=x_scales[:, 0:tokens],
+                in_=grouped[:, 0 : tokens * PACK],
             )
             return x_codes, x_scales
 
@@ -115,45 +122,36 @@ def tile_attention_pa_t_kernel(tc, x, Wq, Wk, rope_cos, rope_sin, out_0, out_1):
                 )
 
         def project_chunk(c, x_mx):
-            back = y_psum.tile([P, 2 * FEATURES], F32, name="y")
-            if has_turned(c):
-                project_turned(x_mx, back[:, FEATURES : 2 * FEATURES], LAST)
-            else:
-                project_straight(x_mx, back[:, FEATURES : 2 * FEATURES], LAST)
-            project_straight(x_mx, back[:, 0:FEATURES], LAST - 1)
-            front = y_psum.tile([P, 2 * FEATURES], F32, name="y")
-            for i in range(2):
-                project_straight(x_mx, front[:, i * FEATURES : (i + 1) * FEATURES], i)
-            return front, back
+            n = CHUNKS[c][2]
+            banks = {}
+            for first in range(n - 2, -1, -2):
+                bank = y_psum.tile([P, 2 * FEATURES], F32, name="y")
+                for i in (first + 1, first):
+                    turned = has_turned(c) and i == n - 1
+                    project = project_turned if turned else project_straight
+                    project(x_mx, bank[:, (i - first) * FEATURES : (i - first + 1) * FEATURES], i)
+                banks[first] = bank
+            return banks
 
         def multiply_straight(y_cols, n, t, products, i):
             nc.vector.tensor_tensor(
-                out=products[:, 0, :, i : i + n, :].rearrange("p g i j -> p i g j"),
-                in0=y_cols.rearrange("p (i g j) -> p i g j", i=n, g=GROUPS),
-                in1=tables[:, 0, t : t + n, :].unsqueeze(2).to_broadcast([P, n, GROUPS, DH]),
-                op=MULT,
-            )
-            nc.vector.tensor_tensor(
-                out=products[:, 1, :, i : i + n, :].rearrange("p g i (a j) -> p i g a j", a=2),
-                in0=y_cols.rearrange("p (i g a j) -> p i g a j", i=n, g=GROUPS, a=2)[:, :, :, ::-1, :],
-                in1=tables[:, 1, t : t + n, :]
-                .rearrange("p i (a j) -> p i a j", a=2)
-                .unsqueeze(2)
-                .to_broadcast([P, n, GROUPS, 2, HALF]),
+                out=products[:, :, i : i + n, :, :].rearrange("p c i g j -> p c (i g j)"),
+                in0=y_cols.unsqueeze(1).to_broadcast([P, 2, n * FEATURES]),
+                in1=tables[:, t // 2, :, 0:n, :].unsqueeze(3).to_broadcast([P, 2, n, GROUPS, DH]),
                 op=MULT,
             )
 
-        def multiply_turned(y_cols, chunk_in_batch):
+        def multiply_turned(y_cols, t):
             prod_t = prod_t_pool.tile([P, 2, 2, P], F32)
             nc.vector.tensor_tensor(
                 out=prod_t[:],
                 in0=y_cols.rearrange("p (o n) -> p o n", o=2).unsqueeze(1).to_broadcast([P, 2, 2, P]),
-                in1=tables_t[:, chunk_in_batch, :, :].unsqueeze(2).to_broadcast([P, 2, 2, P]),
+                in1=tables_t[:, t // CHUNK, :, :].unsqueeze(2).to_broadcast([P, 2, 2, P]),
                 op=MULT,
             )
             return prod_t
 
-        def add_turned(prod_t, res):
+        def add_turned(prod_t, res, i):
             total = sum_psum.tile([P, FEATURES], F32)
             for o in range(2):
                 for c, moving in enumerate((ident, swap)):
@@ -165,10 +163,10 @@ def tile_attention_pa_t_kernel(tc, x, Wq, Wk, rope_cos, rope_sin, out_0, out_1):
                         stop=c == 1,
                         is_transpose=True,
                     )
-            nc.scalar.copy(out=res[:, :, LAST, :], in_=total[:].rearrange("p (g j) -> p g j", g=GROUPS))
+            nc.scalar.copy(out=res[:, :, i, :], in_=total[:].rearrange("p (g j) -> p g j", g=GROUPS))
 
         def transpose_tables():
-            for n2 in range(CHUNKS_PER_BATCH // 2):
+            for n2 in range(TURNED // 2):
                 bank = xt_psum.tile([P, 2, 2 * P], F32, tag="xt")
                 for i in range(2):
                     for plane in range(2):
@@ -182,11 +180,11 @@ def tile_attention_pa_t_kernel(tc, x, Wq, Wk, rope_cos, rope_sin, out_0, out_1):
                 )
 
         def store_chunk(c, res):
-            b, t0 = chunk_place(c)
+            b, t0, n = CHUNKS[c]
             for o, out in enumerate((out_0, out_1)):
                 rows = out[b].rearrange("h (p t) j -> p h t j", t=SLOTS)
                 nc.sync.dma_start(
-                    out=rows[:, :, t0 : t0 + CHUNK, :], in_=res[:, o * HEADS : (o + 1) * HEADS, :, :]
+                    out=rows[:, :, t0 : t0 + n, :], in_=res[:, o * HEADS : (o + 1) * HEADS, 0:n, :]
                 )
 
         ident = const.tile([P, P], F32)
@@ -201,12 +199,16 @@ def tile_attention_pa_t_kernel(tc, x, Wq, Wk, rope_cos, rope_sin, out_0, out_1):
         nc.sync.dma_start(out=wq_sb[:], in_=Wq)
         wk_sb = const.tile([P, D], BF16)
         nc.sync.dma_start(out=wk_sb[:], in_=Wk)
-        x_tiles = [load_chunk(0), load_chunk(1)]
-        tables = const.tile([P, 2, SLOTS, DH], BF16)
-        nc.sync.dma_start(out=tables[:, 0, :, :], in_=rope_cos.rearrange("(p t) j -> p t j", t=SLOTS))
-        nc.sync.dma_start(out=tables[:, 1, :, :], in_=rope_sin.rearrange("(p t) j -> p t j", t=SLOTS))
+        x_tiles = []
+        tables = const.tile([P, SLOTS // 2, 2, 2, DH], BF16)
+        cosine = const.tile([P, SLOTS, DH], BF16)
+        sine = const.tile([P, SLOTS, DH], BF16)
+        load_chunk(0)
+        load_chunk(1)
+        nc.sync.dma_start(out=cosine[:], in_=rope_cos.rearrange("(p t) j -> p t j", t=SLOTS))
+        nc.sync.dma_start(out=sine[:], in_=rope_sin.rearrange("(p t) j -> p t j", t=SLOTS))
         for c in range(2, N_CHUNKS):
-            x_tiles.append(load_chunk(c))
+            load_chunk(c)
 
         w_bank = xt_psum.tile([P, 2, 2 * P], F32, tag="xt")
         transpose_words(w_bank, wq_sb, 0, 0)
@@ -218,52 +220,56 @@ def tile_attention_pa_t_kernel(tc, x, Wq, Wk, rope_cos, rope_sin, out_0, out_1):
         w_scales = const.tile([P, FEATURES], U8, align_bytes=64)
         nc.vector.quantize_mx(out=w_codes[:].bitcast(FP8X4), scales=w_scales[:], in_=w_grouped[:])
 
-        x_mx = quantise_chunk(transpose_chunk(x_tiles[0]))
-        nc.gpsimd.tensor_scalar(
-            out=tables[:, 1, :, 0:HALF], in0=tables[:, 1, :, 0:HALF], scalar1=-1.0, scalar2=0.0, op0=MULT, op1=ADD
-        )
-        spread = const.tile([P, CHUNKS_PER_BATCH, 2, HEADS, DH], F32)
-        last_slots = tables[:].rearrange("p c (n i) j -> p c n i j", i=CHUNK)[:, :, :, LAST, :]
-        for plane, source, target in ((0, 0, 0), (1, 0, HALF), (1, HALF, 0)):
-            width = DH if plane == 0 else HALF
+        x_mx = quantise_chunk(0, transpose_chunk(0))
+        waiting = [transpose_chunk(1), transpose_chunk(2)]
+        y_next = project_chunk(0, x_mx)
+        x_mx = quantise_chunk(1, waiting.pop(0))
+        nc.vector.tensor_copy(out=tables[:, :, 0, :, :], in_=cosine[:].rearrange("p (n i) j -> p n i j", i=2))
+        for a, sign in enumerate((1.0, -1.0)):
+            nc.vector.tensor_scalar(
+                out=tables[:, :, 1, :, a * HALF : (a + 1) * HALF],
+                in0=sine[:, :, (1 - a) * HALF : (2 - a) * HALF].rearrange("p (n i) j -> p n i j", i=2),
+                scalar1=sign,
+                scalar2=None,
+                op0=MULT,
+            )
+        spread = const.tile([P, TURNED, 2, HEADS, DH], F32)
+        last_slots = tables[:, 1 : SLOTS // 2 : 2, :, 1, :]
+        for plane in range(2):
             nc.gpsimd.tensor_scalar(
-                out=spread[:, :, plane, :, target : target + width],
-                in0=last_slots[:, plane, :, source : source + width]
-                .unsqueeze(2)
-                .to_broadcast([P, CHUNKS_PER_BATCH, HEADS, width]),
+                out=spread[:, :, plane, :, :],
+                in0=last_slots[:, :, plane, :].unsqueeze(2).to_broadcast([P, TURNED, HEADS, DH]),
                 scalar1=1.0,
                 scalar2=0.0,
                 op0=MULT,
                 op1=ADD,
             )
-        tables_t = const.tile([P, CHUNKS_PER_BATCH, 2, P], F32)
-        grouped_next = transpose_chunk(x_tiles[1])
-        y_next = project_chunk(0, x_mx)
+        tables_t = const.tile([P, TURNED, 2, P], F32)
         for c in range(N_CHUNKS):
-            if c + 1 < N_CHUNKS:
-                x_mx = quantise_chunk(grouped_next)
-            if c + 2 < N_CHUNKS:
-                grouped_next = transpose_chunk(x_tiles[c + 2])
-            if c == 0:
-                transpose_tables()
-            front, back = y_next
+            t0, n = CHUNKS[c][1:]
+            y_banks = y_next
+            products = prod_pool.tile([P, 2, CHUNK, GROUPS, DH], F32)
+            res = res_pool.tile([P, GROUPS, CHUNK, DH], F32)
+            straight = n - 1 if has_turned(c) else n
+            if 0 < c < N_CHUNKS - 1:
+                x_mx = quantise_chunk(c + 1, waiting.pop(0))
+            if c + AHEAD < N_CHUNKS:
+                waiting.append(transpose_chunk(c + AHEAD))
             if c + 1 < N_CHUNKS:
                 y_next = project_chunk(c + 1, x_mx)
-            products = prod_pool.tile([P, 2, GROUPS, CHUNK, DH], F32)
-            res = res_pool.tile([P, GROUPS, CHUNK, DH], F32)
-            first_slot = chunk_place(c)[1]
-            straight = LAST if has_turned(c) else CHUNK
+            if c == FIRST_TURNED - 2:
+                transpose_tables()
             if has_turned(c):
-                prod_t = multiply_turned(back[:, FEATURES : 2 * FEATURES], c % CHUNKS_PER_BATCH)
-                add_turned(prod_t, res)
-            n_back = straight - 2
-            multiply_straight(back[:, 0 : n_back * FEATURES], n_back, first_slot + 2, products, 2)
-            multiply_straight(front[:], 2, first_slot, products, 0)
+                prod_t = multiply_turned(y_banks[n - 2][:, FEATURES : 2 * FEATURES], t0 + n - 1)
+                add_turned(prod_t, res, n - 1)
+            for first in range(n - 2, -1, -2):
+                width = min(2, straight - first)
+                multiply_straight(y_banks[first][:, 0 : width * FEATURES], width, t0 + first, products, first)
             adder = nc.vector if c == N_CHUNKS - 1 else nc.gpsimd
             adder.tensor_tensor(
-                out=res[:, :, 0:straight, :],
-                in0=products[:, 0, :, 0:straight, :],
-                in1=products[:, 1, :, 0:straight, :],
+                out=res[:, :, 0:straight, :].rearrange("p g i (a j) -> p i g a j", a=2),
+                in0=products[:, 0, 0:straight, :, :].rearrange("p i g (a j) -> p i g a j", a=2),
+                in1=products[:, 1, 0:straight, :, :].rearrange("p i g (a j) -> p i g a j", a=2)[:, :, :, ::-1, :],
                 op=ADD,
             )
             store_chunk(c, res)

@@ -29,6 +29,7 @@ CHUNKS = (
 N_CHUNKS = len(CHUNKS)
 TURNED = SLOTS // CHUNK
 AHEAD = 3
+EARLY_SLOTS = 4
 FIRST_TURNED = 4
 
 FLOPS = 2 * B * S * D * FEATURES
@@ -137,8 +138,18 @@ def tile_attention_pa_t_kernel(tc, x, Wq, Wk, rope_cos, rope_sin, out_0, out_1):
             nc.vector.tensor_tensor(
                 out=products[:, :, i : i + n, :, :].rearrange("p c i g j -> p c (i g j)"),
                 in0=y_cols.unsqueeze(1).to_broadcast([P, 2, n * FEATURES]),
-                in1=tables[:, t // 2, :, 0:n, :].unsqueeze(3).to_broadcast([P, 2, n, GROUPS, DH]),
+                in1=tables[:, t // 2, :, t % 2 : t % 2 + n, :].unsqueeze(3).to_broadcast([P, 2, n, GROUPS, DH]),
                 op=MULT,
+            )
+
+        def add_straight(adder, products, res, i0, i1):
+            cos_part = products[:, 0, i0:i1, :, :].rearrange("p i g (a j) -> p i g a j", a=2)
+            sin_part = products[:, 1, i0:i1, :, :].rearrange("p i g (a j) -> p i g a j", a=2)
+            adder.tensor_tensor(
+                out=res[:, :, i0:i1, :].rearrange("p g i (a j) -> p i g a j", a=2),
+                in0=cos_part,
+                in1=sin_part[:, :, :, ::-1, :],
+                op=ADD,
             )
 
         def multiply_turned(y_cols, t):
@@ -164,6 +175,18 @@ def tile_attention_pa_t_kernel(tc, x, Wq, Wk, rope_cos, rope_sin, out_0, out_1):
                         is_transpose=True,
                     )
             nc.scalar.copy(out=res[:, :, i, :], in_=total[:].rearrange("p (g j) -> p g j", g=GROUPS))
+
+        def spread_tables():
+            last_slots = tables[:, 1 : SLOTS // 2 : 2, :, 1, :]
+            for plane in range(2):
+                nc.gpsimd.tensor_scalar(
+                    out=spread[:, :, plane, :, :],
+                    in0=last_slots[:, :, plane, :].unsqueeze(2).to_broadcast([P, TURNED, HEADS, DH]),
+                    scalar1=1.0,
+                    scalar2=0.0,
+                    op0=MULT,
+                    op1=ADD,
+                )
 
         def transpose_tables():
             for n2 in range(TURNED // 2):
@@ -203,11 +226,39 @@ def tile_attention_pa_t_kernel(tc, x, Wq, Wk, rope_cos, rope_sin, out_0, out_1):
         tables = const.tile([P, SLOTS // 2, 2, 2, DH], BF16)
         cosine = const.tile([P, SLOTS, DH], BF16)
         sine = const.tile([P, SLOTS, DH], BF16)
+
+        def load_tables(t0, t1):
+            for table, source in ((cosine, rope_cos), (sine, rope_sin)):
+                nc.sync.dma_start(out=table[:, t0:t1, :], in_=source.rearrange("(p t) j -> p t j", t=SLOTS)[:, t0:t1, :])
+
+        def table_parts(t0, t1):
+            pairs = slice(t0 // 2, t1 // 2)
+            raw_cos = cosine[:, t0:t1, :].rearrange("p (n i) j -> p n i j", i=2)
+            raw_sin = sine[:, t0:t1, :].rearrange("p (n i) j -> p n i j", i=2)
+            return (
+                (tables[:, pairs, 0, :, :], raw_cos, 1.0),
+                (tables[:, pairs, 1, :, 0:HALF], raw_sin[:, :, :, HALF:DH], 1.0),
+                (tables[:, pairs, 1, :, HALF:DH], raw_sin[:, :, :, 0:HALF], -1.0),
+            )
+
+        def lay_out_early_tables():
+            for target, source, sign in table_parts(0, EARLY_SLOTS):
+                nc.vector.tensor_scalar(out=target, in0=source, scalar1=sign, scalar2=None, op0=MULT)
+
+        def lay_out_late_tables():
+            for target, source, sign in table_parts(EARLY_SLOTS, SLOTS):
+                if sign == 1.0:
+                    nc.scalar.copy(out=target, in_=source)
+                else:
+                    nc.scalar.mul(out=target, in_=source, mul=sign)
+
         load_chunk(0)
+        load_tables(0, EARLY_SLOTS)
         load_chunk(1)
-        nc.sync.dma_start(out=cosine[:], in_=rope_cos.rearrange("(p t) j -> p t j", t=SLOTS))
-        nc.sync.dma_start(out=sine[:], in_=rope_sin.rearrange("(p t) j -> p t j", t=SLOTS))
-        for c in range(2, N_CHUNKS):
+        load_chunk(2)
+        load_chunk(3)
+        load_tables(EARLY_SLOTS, SLOTS)
+        for c in range(4, N_CHUNKS):
             load_chunk(c)
 
         w_bank = xt_psum.tile([P, 2, 2 * P], F32, tag="xt")
@@ -220,30 +271,13 @@ def tile_attention_pa_t_kernel(tc, x, Wq, Wk, rope_cos, rope_sin, out_0, out_1):
         w_scales = const.tile([P, FEATURES], U8, align_bytes=64)
         nc.vector.quantize_mx(out=w_codes[:].bitcast(FP8X4), scales=w_scales[:], in_=w_grouped[:])
 
+        lay_out_early_tables()
         x_mx = quantise_chunk(0, transpose_chunk(0))
         waiting = [transpose_chunk(1), transpose_chunk(2)]
         y_next = project_chunk(0, x_mx)
         x_mx = quantise_chunk(1, waiting.pop(0))
-        nc.vector.tensor_copy(out=tables[:, :, 0, :, :], in_=cosine[:].rearrange("p (n i) j -> p n i j", i=2))
-        for a, sign in enumerate((1.0, -1.0)):
-            nc.vector.tensor_scalar(
-                out=tables[:, :, 1, :, a * HALF : (a + 1) * HALF],
-                in0=sine[:, :, (1 - a) * HALF : (2 - a) * HALF].rearrange("p (n i) j -> p n i j", i=2),
-                scalar1=sign,
-                scalar2=None,
-                op0=MULT,
-            )
+        lay_out_late_tables()
         spread = const.tile([P, TURNED, 2, HEADS, DH], F32)
-        last_slots = tables[:, 1 : SLOTS // 2 : 2, :, 1, :]
-        for plane in range(2):
-            nc.gpsimd.tensor_scalar(
-                out=spread[:, :, plane, :, :],
-                in0=last_slots[:, :, plane, :].unsqueeze(2).to_broadcast([P, TURNED, HEADS, DH]),
-                scalar1=1.0,
-                scalar2=0.0,
-                op0=MULT,
-                op1=ADD,
-            )
         tables_t = const.tile([P, TURNED, 2, P], F32)
         for c in range(N_CHUNKS):
             t0, n = CHUNKS[c][1:]
@@ -253,10 +287,12 @@ def tile_attention_pa_t_kernel(tc, x, Wq, Wk, rope_cos, rope_sin, out_0, out_1):
             straight = n - 1 if has_turned(c) else n
             if 0 < c < N_CHUNKS - 1:
                 x_mx = quantise_chunk(c + 1, waiting.pop(0))
-            if c + AHEAD < N_CHUNKS:
-                waiting.append(transpose_chunk(c + AHEAD))
             if c + 1 < N_CHUNKS:
                 y_next = project_chunk(c + 1, x_mx)
+            if c + AHEAD < N_CHUNKS:
+                waiting.append(transpose_chunk(c + AHEAD))
+            if c == 1:
+                spread_tables()
             if c == FIRST_TURNED - 2:
                 transpose_tables()
             if has_turned(c):
@@ -265,11 +301,5 @@ def tile_attention_pa_t_kernel(tc, x, Wq, Wk, rope_cos, rope_sin, out_0, out_1):
             for first in range(n - 2, -1, -2):
                 width = min(2, straight - first)
                 multiply_straight(y_banks[first][:, 0 : width * FEATURES], width, t0 + first, products, first)
-            adder = nc.vector if c == N_CHUNKS - 1 else nc.gpsimd
-            adder.tensor_tensor(
-                out=res[:, :, 0:straight, :].rearrange("p g i (a j) -> p i g a j", a=2),
-                in0=products[:, 0, 0:straight, :, :].rearrange("p i g (a j) -> p i g a j", a=2),
-                in1=products[:, 1, 0:straight, :, :].rearrange("p i g (a j) -> p i g a j", a=2)[:, :, :, ::-1, :],
-                op=ADD,
-            )
+            add_straight(nc.vector if c == N_CHUNKS - 1 else nc.gpsimd, products, res, 0, straight)
             store_chunk(c, res)

@@ -28,7 +28,7 @@ CHUNKS = (
 )
 N_CHUNKS = len(CHUNKS)
 TURNED = SLOTS // CHUNK
-AHEAD = 3
+AHEAD = 4
 EARLY_SLOTS = 4
 FIRST_TURNED = 4
 
@@ -188,19 +188,16 @@ def tile_attention_pa_t_kernel(tc, x, Wq, Wk, rope_cos, rope_sin, out_0, out_1):
                     op1=ADD,
                 )
 
-        def transpose_tables():
-            for n2 in range(TURNED // 2):
-                bank = xt_psum.tile([P, 2, 2 * P], F32, tag="xt")
-                for i in range(2):
-                    for plane in range(2):
-                        nc.tensor.transpose(
-                            bank[:, i, plane * P : (plane + 1) * P],
-                            spread[:, 2 * n2 + i, plane, :, :].rearrange("p h j -> p (h j)"),
-                            ident[:],
-                        )
-                nc.scalar.copy(
-                    out=tables_t[:, 2 * n2 : 2 * n2 + 2, :, :].rearrange("p n c r -> p n (c r)"), in_=bank[:]
-                )
+        def transpose_tables(n0):
+            bank = xt_psum.tile([P, 2, 2 * P], F32, tag="xt")
+            for i in range(2):
+                for plane in range(2):
+                    nc.tensor.transpose(
+                        bank[:, i, plane * P : (plane + 1) * P],
+                        spread[:, n0 + i, plane, :, :].rearrange("p h j -> p (h j)"),
+                        ident[:],
+                    )
+            nc.scalar.copy(out=tables_t[:, n0 : n0 + 2, :, :].rearrange("p n c r -> p n (c r)"), in_=bank[:])
 
         def store_chunk(c, res):
             b, t0, n = CHUNKS[c]
@@ -289,12 +286,15 @@ def tile_attention_pa_t_kernel(tc, x, Wq, Wk, rope_cos, rope_sin, out_0, out_1):
                 x_mx = quantise_chunk(c + 1, waiting.pop(0))
             if c + 1 < N_CHUNKS:
                 y_next = project_chunk(c + 1, x_mx)
-            if c + AHEAD < N_CHUNKS:
-                waiting.append(transpose_chunk(c + AHEAD))
+            for ahead in range(AHEAD - 1 if c == 0 else AHEAD, AHEAD + 1):
+                if c + ahead < N_CHUNKS:
+                    waiting.append(transpose_chunk(c + ahead))
             if c == 1:
                 spread_tables()
             if c == FIRST_TURNED - 2:
-                transpose_tables()
+                transpose_tables(TURNED // 2)
+            if c == FIRST_TURNED:
+                transpose_tables(0)
             if has_turned(c):
                 prod_t = multiply_turned(y_banks[n - 2][:, FEATURES : 2 * FEATURES], t0 + n - 1)
                 add_turned(prod_t, res, n - 1)

@@ -30,7 +30,7 @@ N_CHUNKS = len(CHUNKS)
 TURNED = SLOTS // CHUNK
 AHEAD = 4
 EARLY_SLOTS = 4
-FIRST_TURNED = 4
+FIRST_TURNED = 6
 
 FLOPS = 2 * B * S * D * FEATURES
 
@@ -179,13 +179,9 @@ def tile_attention_pa_t_kernel(tc, x, Wq, Wk, rope_cos, rope_sin, out_0, out_1):
         def spread_tables():
             last_slots = tables[:, 1 : SLOTS // 2 : 2, :, 1, :]
             for plane in range(2):
-                nc.gpsimd.tensor_scalar(
+                nc.scalar.copy(
                     out=spread[:, :, plane, :, :],
-                    in0=last_slots[:, :, plane, :].unsqueeze(2).to_broadcast([P, TURNED, HEADS, DH]),
-                    scalar1=1.0,
-                    scalar2=0.0,
-                    op0=MULT,
-                    op1=ADD,
+                    in_=last_slots[:, :, plane, :].unsqueeze(2).to_broadcast([P, TURNED, HEADS, DH]),
                 )
 
         def transpose_tables(n0):
@@ -289,12 +285,10 @@ def tile_attention_pa_t_kernel(tc, x, Wq, Wk, rope_cos, rope_sin, out_0, out_1):
             for ahead in range(AHEAD - 1 if c == 0 else AHEAD, AHEAD + 1):
                 if c + ahead < N_CHUNKS:
                     waiting.append(transpose_chunk(c + ahead))
-            if c == 1:
+            if c == FIRST_TURNED - 3:
                 spread_tables()
-            if c == FIRST_TURNED - 2:
-                transpose_tables(TURNED // 2)
-            if c == FIRST_TURNED:
-                transpose_tables(0)
+            if c in (FIRST_TURNED - 2, FIRST_TURNED - 1):
+                transpose_tables((c - FIRST_TURNED + 2) * TURNED // 2)
             if has_turned(c):
                 prod_t = multiply_turned(y_banks[n - 2][:, FEATURES : 2 * FEATURES], t0 + n - 1)
                 add_turned(prod_t, res, n - 1)

from contextlib import ExitStack

import concourse.mybir as mybir
from concourse.masks import make_identity

F32 = mybir.dt.float32
BF16 = mybir.dt.bfloat16
U32 = mybir.dt.uint32
U8 = mybir.dt.uint8
FP8X4 = mybir.dt.float8_e4m3fn_x4
MULT = mybir.AluOpType.mult
ADD = mybir.AluOpType.add

P = 128
PACK = 4
B, S, D = 4, 2048, 512
HEADS, DH = 2, 64
HALF = DH // 2
GROUPS = 2 * HEADS
FEATURES = GROUPS * DH
SLOTS = S // P
WORDS = D // 2
CHUNK = 4
CHUNKS = (
    [(0, t, 2) for t in range(0, 8, 2)]
    + [(b, t, CHUNK) for b in range(B) for t in range(0, SLOTS, CHUNK)][2:-1]
    + [(B - 1, t, 2) for t in (SLOTS - 2, SLOTS - 4)]
)
N_CHUNKS = len(CHUNKS)
TURNED = SLOTS // CHUNK
AHEAD = 4
EARLY_SLOTS = 4
FIRST_TURNED = 6

FLOPS = 2 * B * S * D * FEATURES


def tile_attention_pa_t_kernel(tc, x, Wq, Wk, rope_cos, rope_sin, out_0, out_1):
    nc = tc.nc
    with ExitStack() as stack:
        const = stack.enter_context(tc.tile_pool(name="const", bufs=1))
        x_pool = stack.enter_context(tc.tile_pool(name="x", bufs=N_CHUNKS))
        res_pool = stack.enter_context(tc.tile_pool(name="res", bufs=N_CHUNKS))
        grouped_pool = stack.enter_context(tc.tile_pool(name="grouped", bufs=AHEAD + 1))
        codes_pool = stack.enter_context(tc.tile_pool(name="codes", bufs=2))
        prod_pool = stack.enter_context(tc.tile_pool(name="prod", bufs=3))
        prod_t_pool = stack.enter_context(tc.tile_pool(name="prod_t", bufs=2))
        xt_psum = stack.enter_context(tc.psum_pool(name="xt_psum", bufs=3))
        y_psum = stack.enter_context(tc.psum_pool(name="y_psum", bufs=CHUNK))
        sum_psum = stack.enter_context(tc.psum_pool(name="sum_psum", bufs=1))
        stack.enter_context(tc.manual_schedule())

        def has_turned(c):
            t0, n = CHUNKS[c][1:]
            return c >= FIRST_TURNED and (t0 + n) % CHUNK == 0

        def load_chunk(c):
            b, t0, n = CHUNKS[c]
            x_sb = x_pool.tile([P, CHUNK * D], BF16)
            rows = x[b].rearrange("(p t) d -> p (t d)", t=SLOTS)
            nc.sync.dma_start(out=x_sb[:, 0 : n * D], in_=rows[:, t0 * D : (t0 + n) * D])
            x_tiles.append(x_sb)

        def transpose_words(bank, rows_sb, first_word, column):
            words = rows_sb[:].bitcast(F32)
            for u in range(2):
                nc.tensor.transpose(
                    bank[:, u, column : column + P],
                    words[:, first_word + u : first_word + WORDS : 2],
                    ident[:],
                )

        def transpose_chunk(c):
            grouped = grouped_pool.tile([P, CHUNK * P * PACK], BF16, align_bytes=64)
            grouped_words = grouped[:].bitcast(F32).rearrange("p (n u) -> p n u", u=2)
            for pair in range(CHUNKS[c][2] // 2):
                bank = xt_psum.tile([P, 2, 2 * P], F32, tag="xt")
                for i in range(2):
                    transpose_words(bank, x_tiles[c], (2 * pair + i) * WORDS, i * P)
                nc.scalar.copy(
                    out=grouped_words[:, pair * 2 * P : (pair + 1) * 2 * P, :],
                    in_=bank[:].rearrange("p u n -> p n u"),
                )
            return grouped

        def quantise_chunk(c, grouped):
            x_codes = codes_pool.tile([P, CHUNK * P], U32, align_bytes=64)
            x_scales = codes_pool.tile([P, CHUNK * P], U8, align_bytes=64)
            tokens = CHUNKS[c][2] * P
            nc.vector.quantize_mx(
                out=x_codes[:, 0:tokens].bitcast(FP8X4),
                scales=x_scales[:, 0:tokens],
                in_=grouped[:, 0 : tokens * PACK],
            )
            return x_codes, x_scales

        def project_straight(x_mx, y_cols, i):
            x_codes, x_scales = x_mx
            tokens = slice(i * P, (i + 1) * P)
            nc.tensor.matmul_mx(
                out=y_cols,
                lhsT=x_codes[:, tokens].bitcast(FP8X4),
                lhsT_scale=x_scales[:, tokens],
                rhs=w_codes[:].bitcast(FP8X4),
                rhs_scale=w_scales[:],
                start=True,
                stop=True,
            )

        def project_turned(x_mx, y_cols, i):
            x_codes, x_scales = x_mx
            tokens = slice(i * P, (i + 1) * P)
            for o in range(2):
                rows = slice(o * P, (o + 1) * P)
                nc.tensor.matmul_mx(
                    out=y_cols[:, rows],
                    lhsT=w_codes[:, rows].bitcast(FP8X4),
                    lhsT_scale=w_scales[:, rows],
                    rhs=x_codes[:, tokens].bitcast(FP8X4),
                    rhs_scale=x_scales[:, tokens],
                    start=True,
                    stop=True,
                )

        def project_chunk(c, x_mx):
            n = CHUNKS[c][2]
            banks = {}
            for first in range(n - 2, -1, -2):
                bank = y_psum.tile([P, 2 * FEATURES], F32, name="y")
                for i in (first + 1, first):
                    turned = has_turned(c) and i == n - 1
                    project = project_turned if turned else project_straight
                    project(x_mx, bank[:, (i - first) * FEATURES : (i - first + 1) * FEATURES], i)
                banks[first] = bank
            return banks

        def multiply_straight(y_cols, n, t, products, i):
            nc.vector.tensor_tensor(
                out=products[:, :, i : i + n, :, :].rearrange("p c i g j -> p c (i g j)"),
                in0=y_cols.unsqueeze(1).to_broadcast([P, 2, n * FEATURES]),
                in1=tables[:, t // 2, :, t % 2 : t % 2 + n, :].unsqueeze(3).to_broadcast([P, 2, n, GROUPS, DH]),
                op=MULT,
            )

        def add_straight(adder, products, res, i0, i1):
            cos_part = products[:, 0, i0:i1, :, :].rearrange("p i g (a j) -> p i g a j", a=2)
            sin_part = products[:, 1, i0:i1, :, :].rearrange("p i g (a j) -> p i g a j", a=2)
            adder.tensor_tensor(
                out=res[:, :, i0:i1, :].rearrange("p g i (a j) -> p i g a j", a=2),
                in0=cos_part,
                in1=sin_part[:, :, :, ::-1, :],
                op=ADD,
            )

        def multiply_turned(y_cols, t):
            prod_t = prod_t_pool.tile([P, 2, 2, P], F32)
            nc.vector.tensor_tensor(
                out=prod_t[:],
                in0=y_cols.rearrange("p (o n) -> p o n", o=2).unsqueeze(1).to_broadcast([P, 2, 2, P]),
                in1=tables_t[:, t // CHUNK, :, :].unsqueeze(2).to_broadcast([P, 2, 2, P]),
                op=MULT,
            )
            return prod_t

        def add_turned(prod_t, res, i):
            total = sum_psum.tile([P, FEATURES], F32)
            for o in range(2):
                for c, moving in enumerate((ident, swap)):
                    nc.tensor.matmul(
                        out=total[:, o * P : (o + 1) * P],
                        lhsT=prod_t[:, c, o, :],
                        rhs=moving[:],
                        start=c == 0,
                        stop=c == 1,
                        is_transpose=True,
                    )
            nc.scalar.copy(out=res[:, :, i, :], in_=total[:].rearrange("p (g j) -> p g j", g=GROUPS))

        def spread_tables():
            last_slots = tables[:, 1 : SLOTS // 2 : 2, :, 1, :]
            for plane in range(2):
                nc.scalar.copy(
                    out=spread[:, :, plane, :, :],
                    in_=last_slots[:, :, plane, :].unsqueeze(2).to_broadcast([P, TURNED, HEADS, DH]),
                )

        def transpose_tables(n0):
            bank = xt_psum.tile([P, 2, 2 * P], F32, tag="xt")
            for i in range(2):
                for plane in range(2):
                    nc.tensor.transpose(
                        bank[:, i, plane * P : (plane + 1) * P],
                        spread[:, n0 + i, plane, :, :].rearrange("p h j -> p (h j)"),
                        ident[:],
                    )
            nc.scalar.copy(out=tables_t[:, n0 : n0 + 2, :, :].rearrange("p n c r -> p n (c r)"), in_=bank[:])

        def store_chunk(c, res):
            b, t0, n = CHUNKS[c]
            for o, out in enumerate((out_0, out_1)):
                rows = out[b].rearrange("h (p t) j -> p h t j", t=SLOTS)
                nc.sync.dma_start(
                    out=rows[:, :, t0 : t0 + n, :], in_=res[:, o * HEADS : (o + 1) * HEADS, 0:n, :]
                )

        ident = const.tile([P, P], F32)
        make_identity(nc, ident[:])
        swap = const.tile([P, P], F32)
        for a in range(2):
            nc.gpsimd.tensor_copy(
                out=swap[:].rearrange("p (h a j) -> p h a j", h=HEADS, a=2)[:, :, a, :],
                in_=ident[:].rearrange("p (h a j) -> p h a j", h=HEADS, a=2)[:, :, 1 - a, :],
            )
        wq_sb = const.tile([P, D], BF16)
        nc.sync.dma_start(out=wq_sb[:], in_=Wq)
        wk_sb = const.tile([P, D], BF16)
        nc.sync.dma_start(out=wk_sb[:], in_=Wk)
        x_tiles = []
        tables = const.tile([P, SLOTS // 2, 2, 2, DH], BF16)
        cosine = const.tile([P, SLOTS, DH], BF16)
        sine = const.tile([P, SLOTS, DH], BF16)

        def load_tables(t0, t1):
            for table, source in ((cosine, rope_cos), (sine, rope_sin)):
                nc.sync.dma_start(out=table[:, t0:t1, :], in_=source.rearrange("(p t) j -> p t j", t=SLOTS)[:, t0:t1, :])

        def table_parts(t0, t1):
            pairs = slice(t0 // 2, t1 // 2)
            raw_cos = cosine[:, t0:t1, :].rearrange("p (n i) j -> p n i j", i=2)
            raw_sin = sine[:, t0:t1, :].rearrange("p (n i) j -> p n i j", i=2)
            return (
                (tables[:, pairs, 0, :, :], raw_cos, 1.0),
                (tables[:, pairs, 1, :, 0:HALF], raw_sin[:, :, :, HALF:DH], 1.0),
                (tables[:, pairs, 1, :, HALF:DH], raw_sin[:, :, :, 0:HALF], -1.0),
            )

        def lay_out_early_tables():
            for target, source, sign in table_parts(0, EARLY_SLOTS):
                nc.vector.tensor_scalar(out=target, in0=source, scalar1=sign, scalar2=None, op0=MULT)

        def lay_out_late_tables():
            for target, source, sign in table_parts(EARLY_SLOTS, SLOTS):
                if sign == 1.0:
                    nc.scalar.copy(out=target, in_=source)
                else:
                    nc.scalar.mul(out=target, in_=source, mul=sign)

        load_chunk(0)
        load_tables(0, EARLY_SLOTS)
        load_chunk(1)
        load_chunk(2)
        load_chunk(3)
        load_tables(EARLY_SLOTS, SLOTS)
        for c in range(4, N_CHUNKS):
            load_chunk(c)

        w_bank = xt_psum.tile([P, 2, 2 * P], F32, tag="xt")
        transpose_words(w_bank, wq_sb, 0, 0)
        transpose_words(w_bank, wk_sb, 0, P)
        w_grouped = const.tile([P, FEATURES * PACK], BF16, align_bytes=64)
        w_words = w_grouped[:].bitcast(F32).rearrange("p (n u) -> p n u", u=2)
        nc.vector.tensor_copy(out=w_words, in_=w_bank[:].rearrange("p u n -> p n u"))
        w_codes = const.tile([P, FEATURES], U32, align_bytes=64)
        w_scales = const.tile([P, FEATURES], U8, align_bytes=64)
        nc.vector.quantize_mx(out=w_codes[:].bitcast(FP8X4), scales=w_scales[:], in_=w_grouped[:])

        lay_out_early_tables()
        x_mx = quantise_chunk(0, transpose_chunk(0))
        waiting = [transpose_chunk(1), transpose_chunk(2)]
        y_next = project_chunk(0, x_mx)
        x_mx = quantise_chunk(1, waiting.pop(0))
        lay_out_late_tables()
        spread = const.tile([P, TURNED, 2, HEADS, DH], F32)
        tables_t = const.tile([P, TURNED, 2, P], F32)
        for c in range(N_CHUNKS):
            t0, n = CHUNKS[c][1:]
            y_banks = y_next
            products = prod_pool.tile([P, 2, CHUNK, GROUPS, DH], F32)
            res = res_pool.tile([P, GROUPS, CHUNK, DH], F32)
            straight = n - 1 if has_turned(c) else n
            if 0 < c < N_CHUNKS - 1:
                x_mx = quantise_chunk(c + 1, waiting.pop(0))
            if c + 1 < N_CHUNKS:
                y_next = project_chunk(c + 1, x_mx)
            for ahead in range(AHEAD - 1 if c == 0 else AHEAD, AHEAD + 1):
                if c + ahead < N_CHUNKS:
                    waiting.append(transpose_chunk(c + ahead))
            if c == FIRST_TURNED - 3:
                spread_tables()
            if c in (FIRST_TURNED - 2, FIRST_TURNED - 1):
                transpose_tables((c - FIRST_TURNED + 2) * TURNED // 2)
            if has_turned(c):
                prod_t = multiply_turned(y_banks[n - 2][:, FEATURES : 2 * FEATURES], t0 + n - 1)
                add_turned(prod_t, res, n - 1)
            for first in range(n - 2, -1, -2):
                width = min(2, straight - first)
                multiply_straight(y_banks[first][:, 0 : width * FEATURES], width, t0 + first, products, first)
            add_straight(nc.vector if c == N_CHUNKS - 1 else nc.gpsimd, products, res, 0, straight)
            store_chunk(c, res)
